import numpy as np
import ml_dtypes


def mxq(x, axis, fmt="e4m3"):
    dtype, down = {"e4m3": (ml_dtypes.float8_e4m3fn, 7), "e5m2": (ml_dtypes.float8_e5m2, 14)}[fmt]
    v = np.moveaxis(np.asarray(x, np.float32).astype(ml_dtypes.bfloat16).astype(np.float64), axis, -1)
    blocks = v.reshape(v.shape[:-1] + (-1, 32))
    amax = np.abs(blocks).max(-1, keepdims=True)
    byte = np.maximum(np.where(amax > 0, np.frexp(amax)[1] - 1 + 127, 0) - down, 1)
    scale = np.exp2(byte - 127.0)
    codes = (blocks / scale).astype(np.float32).astype(dtype).astype(np.float64)
    return np.moveaxis((codes * scale).reshape(v.shape), -1, axis)


WIDE = False


def mx_kscale(k):
    if not WIDE:
        return np.ones(k)
    levels = np.array([10, -10, 5, -5, 0])
    a = np.random.permutation(np.resize(levels, k // 512 * 4)).reshape(k // 512, 4)
    idx = np.arange(k)
    return np.exp2(a[idx // 512, idx % 128 // 32])


BF16 = ml_dtypes.bfloat16


def bf(x):
    return np.asarray(x, np.float32).astype(BF16)


def f64(x):
    return np.asarray(x).astype(np.float64)


NB, D, CO, CV, R = 16, 256, 128, 512, 512


def setup_inputs():
    s, t = mx_kscale(CV), mx_kscale(R)
    return {"x1": bf(np.random.standard_normal((NB, D, CO))),
            "A": bf(np.random.standard_normal((D, R)) / np.sqrt(D) * t),
            "t2": bf(np.random.standard_normal((NB, R, CV)) * s),
            "w": bf(np.random.standard_normal((NB, CO, CV)) / np.sqrt(CV) / s),
            "C": bf(np.random.standard_normal((D, R)) / np.sqrt(R) / t)}


def reference(x1, A, t2, w, C):
    t1 = f64(A).T @ f64(x1)
    t3 = mxq(f64(t2), 2, "e4m3") @ mxq(f64(w).transpose(0, 2, 1), 1, "e4m3")
    h = t1 * t3
    return mxq(f64(C), 1, "e4m3") @ mxq(h, 1, "e4m3")

@@ -1,0 +1,255 @@
+from contextlib import ExitStack
+
+import concourse.mybir as mybir
+from concourse.masks import make_identity
+
+F32 = mybir.dt.float32
+BF16 = mybir.dt.bfloat16
+U32 = mybir.dt.uint32
+U8 = mybir.dt.uint8
+FP8X4 = mybir.dt.float8_e4m3fn_x4
+
+NB, D, CO, CV, R = 16, 256, 128, 512, 512
+P = 128
+PACK = 4
+HALVES = 2
+D_ROWS = D // P
+PAIR = 2
+GROUP = 4
+
+FLOPS = 2 * NB * R * CO * (D + CV) + 2 * NB * D * CO * R
+
+AT_PROJECT = 0
+AT_TRANSPOSE = 2
+AT_QUANTISE = 3
+AT_T3 = 4
+AT_MULTIPLY = 5
+AT_QUANTISE_H = 6
+AT_OUT = 7
+
+
+def tile_cptensorproduct_pa_kernel(tc, x1, A, t2, w, C, out):
+    nc = tc.nc
+    with ExitStack() as ctx:
+        consts = ctx.enter_context(tc.tile_pool(name="consts", bufs=1))
+        x1_pool = ctx.enter_context(tc.tile_pool(name="x1_pool", bufs=NB // GROUP))
+        w_pool = ctx.enter_context(tc.tile_pool(name="w_pool", bufs=NB // PAIR))
+        t2_pool = ctx.enter_context(tc.tile_pool(name="t2_pool", bufs=NB))
+        work = ctx.enter_context(tc.tile_pool(name="work", bufs=3))
+        t1_pool = ctx.enter_context(tc.tile_pool(name="t1_pool", bufs=8))
+        out_pool = ctx.enter_context(tc.tile_pool(name="out_pool", bufs=NB // PAIR))
+        tr_psum = ctx.enter_context(tc.psum_pool(name="tr_psum", bufs=4))
+        t1_psum = ctx.enter_context(tc.psum_pool(name="t1_psum", bufs=1))
+        t3_psum = ctx.enter_context(tc.psum_pool(name="t3_psum", bufs=2))
+        out_psum = ctx.enter_context(tc.psum_pool(name="out_psum", bufs=1))
+
+        c_in = consts.tile([P, D_ROWS * R], BF16)
+        nc.sync.dma_start(out=c_in[:], in_=C.rearrange("(p i) r -> p (i r)", i=D_ROWS))
+        a_in = consts.tile([P, D_ROWS * R], BF16)
+        nc.sync.dma_start(out=a_in[:], in_=A.rearrange("(p i) r -> p (i r)", i=D_ROWS))
+
+        x1_tiles = []
+        w_tiles = []
+        t2_tiles = []
+
+        def load_x1(g):
+            x1_in = x1_pool.tile([P, GROUP, D_ROWS * CO], BF16)
+            nc.sync.dma_start(
+                out=x1_in[:],
+                in_=x1[g * GROUP : (g + 1) * GROUP].rearrange("b (p i) c -> p b (i c)", i=D_ROWS),
+            )
+            x1_tiles.append(x1_in)
+
+        load_x1(0)
+        for q in range(NB // PAIR):
+            if q % 2 == 1 and (q + 1) // 2 < NB // GROUP:
+                load_x1((q + 1) // 2)
+            w_in = w_pool.tile([P, PAIR, CV], BF16)
+            nc.sync.dma_start(out=w_in[:], in_=w[q * PAIR : (q + 1) * PAIR].rearrange("s o v -> o s v"))
+            w_tiles.append(w_in)
+            for s in range(PAIR):
+                t2_in = t2_pool.tile([P, PACK * CV], BF16)
+                nc.sync.dma_start(
+                    out=t2_in[:], in_=t2[q * PAIR + s].rearrange("(p j) v -> p (j v)", j=PACK)
+                )
+                t2_tiles.append(t2_in)
+
+        ident = consts.tile([P, P], F32)
+        make_identity(nc, ident[:])
+
+        c_words = c_in[:].bitcast(F32)
+        cT_ps = tr_psum.tile([P, D_ROWS, HALVES, P], F32, tag="tr")
+        for i in range(D_ROWS):
+            for u in range(HALVES):
+                nc.tensor.transpose(
+                    cT_ps[:, i, u, :],
+                    c_words[:, i * (R // 2) + u : (i + 1) * (R // 2) : 2],
+                    ident[:],
+                )
+        c_grouped = consts.tile([P, D_ROWS * P * PACK], BF16, align_bytes=64)
+        nc.vector.tensor_copy(
+            out=c_grouped[:].bitcast(F32).rearrange("p (i d u) -> p i d u", i=D_ROWS, u=HALVES),
+            in_=cT_ps[:].rearrange("p i u d -> p i d u"),
+        )
+
+        a_chunks = consts.tile([P, D_ROWS, PACK, P], BF16)
+        nc.vector.tensor_copy(
+            out=a_chunks[:],
+            in_=a_in[:].rearrange("p (i m j) -> p i j m", i=D_ROWS, j=PACK),
+        )
+
+        c_codes = consts.tile([P, D_ROWS * P], U32, align_bytes=64)
+        c_scales = consts.tile([P, D_ROWS * P], U8, align_bytes=64)
+        nc.vector.quantize_mx(out=c_codes[:].bitcast(FP8X4), scales=c_scales[:], in_=c_grouped[:])
+
+        t1_tiles = {}
+        t2_grouped_tiles = {}
+        w_grouped_tiles = {}
+        t2_mx = {}
+        w_mx = {}
+        t3_tiles = {}
+        h_grouped_tiles = {}
+        h_mx = {}
+
+        def project(b):
+            x1_b = x1_tiles[b // GROUP][:, b % GROUP, :]
+            t1_ps = t1_psum.tile([P, PACK, CO], F32)
+            for j in range(PACK):
+                for i in range(D_ROWS):
+                    nc.tensor.matmul(
+                        out=t1_ps[:, j, :],
+                        lhsT=a_chunks[:, i, j, :],
+                        rhs=x1_b[:, i * CO : (i + 1) * CO],
+                        start=(i == 0),
+                        stop=(i == D_ROWS - 1),
+                    )
+            t1_sb = t1_pool.tile([P, CO, PACK], F32)
+            nc.scalar.copy(out=t1_sb[:], in_=t1_ps[:].rearrange("p j c -> p c j"))
+            t1_tiles[b] = t1_sb
+
+        def transpose_operands(b):
+            if b % PAIR == 0:
+                w_words = w_tiles[b // PAIR][:].rearrange("p s v -> p (s v)").bitcast(F32)
+                wT_ps = tr_psum.tile([P, PAIR, HALVES, CO], F32, tag="tr")
+                for s in range(PAIR):
+                    for u in range(HALVES):
+                        k = s * HALVES + u
+                        nc.tensor.transpose(wT_ps[:, s, u, :], w_words[:, k * P : (k + 1) * P], ident[:])
+                w_grouped = work.tile([P, PAIR * CO * PACK], BF16, align_bytes=64)
+                nc.vector.tensor_copy(
+                    out=w_grouped[:].bitcast(F32).rearrange("p (s c u) -> p s c u", s=PAIR, u=HALVES),
+                    in_=wT_ps[:].rearrange("p s u c -> p s c u"),
+                )
+                w_grouped_tiles[b // PAIR] = w_grouped
+
+            t2_words = t2_tiles[b][:].bitcast(F32)
+            t2_grouped = work.tile([P, PACK * P * PACK], BF16, align_bytes=64)
+            grouped_words = t2_grouped[:].bitcast(F32).rearrange("p (j m u) -> p j m u", j=PACK, u=HALVES)
+            for half_bank in range(PACK // 2):
+                t2T_ps = tr_psum.tile([P, 2, HALVES, P], F32, tag="tr")
+                for jj in range(2):
+                    for u in range(HALVES):
+                        k = (half_bank * 2 + jj) * HALVES + u
+                        nc.tensor.transpose(t2T_ps[:, jj, u, :], t2_words[:, k * P : (k + 1) * P], ident[:])
+                nc.scalar.copy(
+                    out=grouped_words[:, half_bank * 2 : half_bank * 2 + 2],
+                    in_=t2T_ps[:].rearrange("p jj u m -> p jj m u"),
+                )
+            t2_grouped_tiles[b] = t2_grouped
+
+        def quantise_operands(b):
+            t2_codes = work.tile([P, PACK * P], U32, align_bytes=64)
+            t2_scales = work.tile([P, PACK * P], U8, align_bytes=64)
+            nc.vector.quantize_mx(
+                out=t2_codes[:].bitcast(FP8X4), scales=t2_scales[:], in_=t2_grouped_tiles[b][:]
+            )
+            t2_mx[b] = (t2_codes, t2_scales)
+            if b % PAIR == 0:
+                w_codes = work.tile([P, PAIR * CO], U32, align_bytes=64)
+                w_scales = work.tile([P, PAIR * CO], U8, align_bytes=64)
+                nc.vector.quantize_mx(
+                    out=w_codes[:].bitcast(FP8X4), scales=w_scales[:], in_=w_grouped_tiles[b // PAIR][:]
+                )
+                w_mx[b // PAIR] = (w_codes, w_scales)
+
+        def contract_channels(b):
+            t2_codes, t2_scales = t2_mx[b]
+            w_codes, w_scales = w_mx[b // PAIR]
+            w_cols = slice((b % PAIR) * CO, (b % PAIR + 1) * CO)
+            t3_ps = t3_psum.tile([P, PACK, CO], F32)
+            for j in range(PACK):
+                ranks = slice(j * P, (j + 1) * P)
+                nc.tensor.matmul_mx(
+                    out=t3_ps[:, j, :],
+                    lhsT=t2_codes[:, ranks].bitcast(FP8X4),
+                    lhsT_scale=t2_scales[:, ranks],
+                    rhs=w_codes[:, w_cols].bitcast(FP8X4),
+                    rhs_scale=w_scales[:, w_cols],
+                    start=True,
+                    stop=True,
+                )
+            t3_tiles[b] = t3_ps
+
+        def multiply(b):
+            if b % PAIR == 0:
+                h_grouped = work.tile([P, PAIR, CO, PACK], BF16, align_bytes=64)
+                h_grouped_tiles[b // PAIR] = h_grouped
+            nc.vector.tensor_tensor(
+                out=h_grouped_tiles[b // PAIR][:, b % PAIR],
+                in0=t1_tiles[b][:],
+                in1=t3_tiles[b][:].rearrange("p j c -> p c j"),
+                op=mybir.AluOpType.mult,
+            )
+
+        def quantise_h(q):
+            h_codes = work.tile([P, PAIR * CO], U32, align_bytes=64)
+            h_scales = work.tile([P, PAIR * CO], U8, align_bytes=64)
+            nc.vector.quantize_mx(
+                out=h_codes[:].bitcast(FP8X4),
+                scales=h_scales[:],
+                in_=h_grouped_tiles[q][:].rearrange("p s c t -> p (s c t)"),
+            )
+            h_mx[q] = (h_codes, h_scales)
+
+        def contract_ranks(q):
+            h_codes, h_scales = h_mx[q]
+            out_ps = out_psum.tile([P, D_ROWS, PAIR * CO], F32)
+            for i in range(D_ROWS):
+                comps = slice(i * P, (i + 1) * P)
+                nc.tensor.matmul_mx(
+                    out=out_ps[:, i, :],
+                    lhsT=c_codes[:, comps].bitcast(FP8X4),
+                    lhsT_scale=c_scales[:, comps],
+                    rhs=h_codes[:].bitcast(FP8X4),
+                    rhs_scale=h_scales[:],
+                    start=True,
+                    stop=True,
+                )
+            out_sb = out_pool.tile([P, PAIR, D_ROWS, CO], F32)
+            nc.scalar.copy(out=out_sb[:], in_=out_ps[:].rearrange("p i (s c) -> p s i c", s=PAIR))
+            nc.sync.dma_start(
+                out=out[q * PAIR : (q + 1) * PAIR].rearrange("s (p i) c -> p s (i c)", i=D_ROWS),
+                in_=out_sb[:].rearrange("p s i c -> p s (i c)"),
+            )
+
+        def is_sample(b):
+            return 0 <= b < NB
+
+        def closes_pair(b):
+            return is_sample(b) and b % PAIR == PAIR - 1
+
+        for n in range(NB + AT_OUT):
+            if is_sample(n - AT_MULTIPLY):
+                multiply(n - AT_MULTIPLY)
+            if is_sample(n - AT_TRANSPOSE):
+                transpose_operands(n - AT_TRANSPOSE)
+            if is_sample(n - AT_PROJECT):
+                project(n - AT_PROJECT)
+            if is_sample(n - AT_QUANTISE):
+                quantise_operands(n - AT_QUANTISE)
+            if is_sample(n - AT_T3):
+                contract_channels(n - AT_T3)
+            if closes_pair(n - AT_QUANTISE_H):
+                quantise_h((n - AT_QUANTISE_H) // PAIR)
+            if closes_pair(n - AT_OUT):
+                contract_ranks((n - AT_OUT) // PAIR)

@@ -43,6 +43,8 @@ def tile_cptensorproduct_pa_kernel(tc, x1, A, t2, w, C, out):
         t3_psum = ctx.enter_context(tc.psum_pool(name="t3_psum", bufs=2))
         out_psum = ctx.enter_context(tc.psum_pool(name="out_psum", bufs=1))
 
+        ctx.enter_context(tc.manual_schedule())
+
         c_in = consts.tile([P, D_ROWS * R], BF16)
         nc.sync.dma_start(out=c_in[:], in_=C.rearrange("(p i) r -> p (i r)", i=D_ROWS))
         a_in = consts.tile([P, D_ROWS * R], BF16)

@@ -16,16 +16,18 @@ HALVES = 2
 D_ROWS = D // P
 PAIR = 2
 GROUP = 4
+PSUM_BANKS = 8
 
 FLOPS = 2 * NB * R * CO * (D + CV) + 2 * NB * D * CO * R
 
 AT_PROJECT = 0
-AT_TRANSPOSE = 2
-AT_QUANTISE = 3
-AT_T3 = 4
-AT_MULTIPLY = 5
-AT_QUANTISE_H = 6
-AT_OUT = 7
+AT_TRANSPOSE = 3
+AT_QUANTISE = 4
+AT_T3 = 5
+AT_MULTIPLY = 6
+AT_QUANTISE_H = 7
+AT_OUT = 8
+ROUND_OF_C = 4
 
 
 def tile_cptensorproduct_pa_kernel(tc, x1, A, t2, w, C, out):
@@ -33,66 +35,52 @@ def tile_cptensorproduct_pa_kernel(tc, x1, A, t2, w, C, out):
     with ExitStack() as ctx:
         consts = ctx.enter_context(tc.tile_pool(name="consts", bufs=1))
         x1_pool = ctx.enter_context(tc.tile_pool(name="x1_pool", bufs=NB // GROUP))
-        w_pool = ctx.enter_context(tc.tile_pool(name="w_pool", bufs=NB // PAIR))
+        w_pool = ctx.enter_context(tc.tile_pool(name="w_pool", bufs=NB // GROUP))
         t2_pool = ctx.enter_context(tc.tile_pool(name="t2_pool", bufs=NB))
         work = ctx.enter_context(tc.tile_pool(name="work", bufs=3))
-        t1_pool = ctx.enter_context(tc.tile_pool(name="t1_pool", bufs=8))
+        t1_pool = ctx.enter_context(tc.tile_pool(name="t1_pool", bufs=AT_MULTIPLY - AT_PROJECT + 2))
         out_pool = ctx.enter_context(tc.tile_pool(name="out_pool", bufs=NB // PAIR))
-        tr_psum = ctx.enter_context(tc.psum_pool(name="tr_psum", bufs=4))
-        t1_psum = ctx.enter_context(tc.psum_pool(name="t1_psum", bufs=1))
-        t3_psum = ctx.enter_context(tc.psum_pool(name="t3_psum", bufs=2))
-        out_psum = ctx.enter_context(tc.psum_pool(name="out_psum", bufs=1))
+        psum = ctx.enter_context(tc.psum_pool(name="psum", bufs=PSUM_BANKS))
 
         ctx.enter_context(tc.manual_schedule())
 
-        c_in = consts.tile([P, D_ROWS * R], BF16)
-        nc.sync.dma_start(out=c_in[:], in_=C.rearrange("(p i) r -> p (i r)", i=D_ROWS))
-        a_in = consts.tile([P, D_ROWS * R], BF16)
-        nc.sync.dma_start(out=a_in[:], in_=A.rearrange("(p i) r -> p (i r)", i=D_ROWS))
+        def is_sample(b):
+            return 0 <= b < NB
 
         x1_tiles = []
         w_tiles = []
         t2_tiles = []
+        w_rows = w.rearrange("b o v -> (b o) v")
 
-        def load_x1(g):
-            x1_in = x1_pool.tile([P, GROUP, D_ROWS * CO], BF16)
-            nc.sync.dma_start(
-                out=x1_in[:],
-                in_=x1[g * GROUP : (g + 1) * GROUP].rearrange("b (p i) c -> p b (i c)", i=D_ROWS),
-            )
-            x1_tiles.append(x1_in)
-
-        load_x1(0)
-        for q in range(NB // PAIR):
-            if q % 2 == 1 and (q + 1) // 2 < NB // GROUP:
-                load_x1((q + 1) // 2)
-            w_in = w_pool.tile([P, PAIR, CV], BF16)
-            nc.sync.dma_start(out=w_in[:], in_=w[q * PAIR : (q + 1) * PAIR].rearrange("s o v -> o s v"))
-            w_tiles.append(w_in)
-            for s in range(PAIR):
-                t2_in = t2_pool.tile([P, PACK * CV], BF16)
+        a_in = consts.tile([P, D_ROWS * R], BF16)
+        nc.sync.dma_start(out=a_in[:], in_=A.rearrange("(p i) r -> p (i r)", i=D_ROWS))
+        c_in = consts.tile([P, D_ROWS * R], BF16)
+        for n in range(NB + AT_TRANSPOSE):
+            if is_sample(n - AT_PROJECT) and (n - AT_PROJECT) % GROUP == 0:
+                b = n - AT_PROJECT
+                x1_in = x1_pool.tile([P, GROUP, D_ROWS * CO], BF16)
                 nc.sync.dma_start(
-                    out=t2_in[:], in_=t2[q * PAIR + s].rearrange("(p j) v -> p (j v)", j=PACK)
+                    out=x1_in[:],
+                    in_=x1[b : b + GROUP].rearrange("b (p i) c -> p b (i c)", i=D_ROWS),
                 )
+                x1_tiles.append(x1_in)
+            if n == ROUND_OF_C:
+                nc.sync.dma_start(out=c_in[:], in_=C.rearrange("(p i) r -> p (i r)", i=D_ROWS))
+            if is_sample(n - AT_TRANSPOSE):
+                b = n - AT_TRANSPOSE
+                if b % GROUP == 0:
+                    w_in = w_pool.tile([P, PACK * CV], BF16)
+                    nc.sync.dma_start(
+                        out=w_in[:],
+                        in_=w_rows[b * CO : (b + GROUP) * CO].rearrange("(p i) v -> p (i v)", i=PACK),
+                    )
+                    w_tiles.append(w_in)
+                t2_in = t2_pool.tile([P, PACK * CV], BF16)
+                nc.sync.dma_start(out=t2_in[:], in_=t2[b].rearrange("(p j) v -> p (j v)", j=PACK))
                 t2_tiles.append(t2_in)
 
         ident = consts.tile([P, P], F32)
         make_identity(nc, ident[:])
-
-        c_words = c_in[:].bitcast(F32)
-        cT_ps = tr_psum.tile([P, D_ROWS, HALVES, P], F32, tag="tr")
-        for i in range(D_ROWS):
-            for u in range(HALVES):
-                nc.tensor.transpose(
-                    cT_ps[:, i, u, :],
-                    c_words[:, i * (R // 2) + u : (i + 1) * (R // 2) : 2],
-                    ident[:],
-                )
-        c_grouped = consts.tile([P, D_ROWS * P * PACK], BF16, align_bytes=64)
-        nc.vector.tensor_copy(
-            out=c_grouped[:].bitcast(F32).rearrange("p (i d u) -> p i d u", i=D_ROWS, u=HALVES),
-            in_=cT_ps[:].rearrange("p i u d -> p i d u"),
-        )
 
         a_chunks = consts.tile([P, D_ROWS, PACK, P], BF16)
         nc.vector.tensor_copy(
@@ -100,9 +88,9 @@ def tile_cptensorproduct_pa_kernel(tc, x1, A, t2, w, C, out):
             in_=a_in[:].rearrange("p (i m j) -> p i j m", i=D_ROWS, j=PACK),
         )
 
+        c_grouped = consts.tile([P, D_ROWS * P * PACK], BF16, align_bytes=64)
         c_codes = consts.tile([P, D_ROWS * P], U32, align_bytes=64)
         c_scales = consts.tile([P, D_ROWS * P], U8, align_bytes=64)
-        nc.vector.quantize_mx(out=c_codes[:].bitcast(FP8X4), scales=c_scales[:], in_=c_grouped[:])
 
         t1_tiles = {}
         t2_grouped_tiles = {}
@@ -113,9 +101,27 @@ def tile_cptensorproduct_pa_kernel(tc, x1, A, t2, w, C, out):
         h_grouped_tiles = {}
         h_mx = {}
 
+        def transpose_c():
+            c_words = c_in[:].bitcast(F32)
+            cT_ps = psum.tile([P, D_ROWS, HALVES, P], F32, tag="bank")
+            for i in range(D_ROWS):
+                for u in range(HALVES):
+                    nc.tensor.transpose(
+                        cT_ps[:, i, u, :],
+                        c_words[:, i * (R // 2) + u : (i + 1) * (R // 2) : 2],
+                        ident[:],
+                    )
+            nc.vector.tensor_copy(
+                out=c_grouped[:].bitcast(F32).rearrange("p (i d u) -> p i d u", i=D_ROWS, u=HALVES),
+                in_=cT_ps[:].rearrange("p i u d -> p i d u"),
+            )
+
+        def quantise_c():
+            nc.vector.quantize_mx(out=c_codes[:].bitcast(FP8X4), scales=c_scales[:], in_=c_grouped[:])
+
         def project(b):
             x1_b = x1_tiles[b // GROUP][:, b % GROUP, :]
-            t1_ps = t1_psum.tile([P, PACK, CO], F32)
+            t1_ps = psum.tile([P, PACK, CO], F32, tag="bank")
             for j in range(PACK):
                 for i in range(D_ROWS):
                     nc.tensor.matmul(
@@ -129,56 +135,59 @@ def tile_cptensorproduct_pa_kernel(tc, x1, A, t2, w, C, out):
             nc.scalar.copy(out=t1_sb[:], in_=t1_ps[:].rearrange("p j c -> p c j"))
             t1_tiles[b] = t1_sb
 
-        def transpose_operands(b):
-            if b % PAIR == 0:
-                w_words = w_tiles[b // PAIR][:].rearrange("p s v -> p (s v)").bitcast(F32)
-                wT_ps = tr_psum.tile([P, PAIR, HALVES, CO], F32, tag="tr")
-                for s in range(PAIR):
+        def transpose_w(g):
+            w_words = w_tiles[g][:].bitcast(F32)
+            w_grouped = work.tile([P, GROUP * CO * PACK], BF16, align_bytes=64)
+            grouped_words = w_grouped[:].bitcast(F32).rearrange("p (q i u) -> p q i u", i=PACK, u=HALVES)
+            for k in range(PACK // 2):
+                wT_ps = psum.tile([P, 2, HALVES, P], F32, tag="bank")
+                for ii in range(2):
                     for u in range(HALVES):
-                        k = s * HALVES + u
-                        nc.tensor.transpose(wT_ps[:, s, u, :], w_words[:, k * P : (k + 1) * P], ident[:])
-                w_grouped = work.tile([P, PAIR * CO * PACK], BF16, align_bytes=64)
+                        first = ((2 * k + ii) * HALVES + u) * P
+                        nc.tensor.transpose(wT_ps[:, ii, u, :], w_words[:, first : first + P], ident[:])
                 nc.vector.tensor_copy(
-                    out=w_grouped[:].bitcast(F32).rearrange("p (s c u) -> p s c u", s=PAIR, u=HALVES),
-                    in_=wT_ps[:].rearrange("p s u c -> p s c u"),
+                    out=grouped_words[:, :, 2 * k : 2 * k + 2, :],
+                    in_=wT_ps[:].rearrange("p ii u q -> p q ii u"),
                 )
-                w_grouped_tiles[b // PAIR] = w_grouped
+            w_grouped_tiles[g] = w_grouped
 
+        def transpose_t2(b):
             t2_words = t2_tiles[b][:].bitcast(F32)
             t2_grouped = work.tile([P, PACK * P * PACK], BF16, align_bytes=64)
             grouped_words = t2_grouped[:].bitcast(F32).rearrange("p (j m u) -> p j m u", j=PACK, u=HALVES)
-            for half_bank in range(PACK // 2):
-                t2T_ps = tr_psum.tile([P, 2, HALVES, P], F32, tag="tr")
+            for k in range(PACK // 2):
+                t2T_ps = psum.tile([P, 2, HALVES, P], F32, tag="bank")
                 for jj in range(2):
                     for u in range(HALVES):
-                        k = (half_bank * 2 + jj) * HALVES + u
-                        nc.tensor.transpose(t2T_ps[:, jj, u, :], t2_words[:, k * P : (k + 1) * P], ident[:])
+                        first = ((2 * k + jj) * HALVES + u) * P
+                        nc.tensor.transpose(t2T_ps[:, jj, u, :], t2_words[:, first : first + P], ident[:])
                 nc.scalar.copy(
-                    out=grouped_words[:, half_bank * 2 : half_bank * 2 + 2],
+                    out=grouped_words[:, 2 * k : 2 * k + 2],
                     in_=t2T_ps[:].rearrange("p jj u m -> p jj m u"),
                 )
             t2_grouped_tiles[b] = t2_grouped
 
-        def quantise_operands(b):
+        def quantise_t2(b):
             t2_codes = work.tile([P, PACK * P], U32, align_bytes=64)
             t2_scales = work.tile([P, PACK * P], U8, align_bytes=64)
             nc.vector.quantize_mx(
                 out=t2_codes[:].bitcast(FP8X4), scales=t2_scales[:], in_=t2_grouped_tiles[b][:]
             )
             t2_mx[b] = (t2_codes, t2_scales)
-            if b % PAIR == 0:
-                w_codes = work.tile([P, PAIR * CO], U32, align_bytes=64)
-                w_scales = work.tile([P, PAIR * CO], U8, align_bytes=64)
-                nc.vector.quantize_mx(
-                    out=w_codes[:].bitcast(FP8X4), scales=w_scales[:], in_=w_grouped_tiles[b // PAIR][:]
-                )
-                w_mx[b // PAIR] = (w_codes, w_scales)
+
+        def quantise_w(g):
+            w_codes = work.tile([P, GROUP * CO], U32, align_bytes=64)
+            w_scales = work.tile([P, GROUP * CO], U8, align_bytes=64)
+            nc.vector.quantize_mx(
+                out=w_codes[:].bitcast(FP8X4), scales=w_scales[:], in_=w_grouped_tiles[g][:]
+            )
+            w_mx[g] = (w_codes, w_scales)
 
         def contract_channels(b):
             t2_codes, t2_scales = t2_mx[b]
-            w_codes, w_scales = w_mx[b // PAIR]
-            w_cols = slice((b % PAIR) * CO, (b % PAIR + 1) * CO)
-            t3_ps = t3_psum.tile([P, PACK, CO], F32)
+            w_codes, w_scales = w_mx[b // GROUP]
+            w_cols = slice((b % GROUP) * CO, (b % GROUP + 1) * CO)
+            t3_ps = psum.tile([P, PACK, CO], F32, tag="bank")
             for j in range(PACK):
                 ranks = slice(j * P, (j + 1) * P)
                 nc.tensor.matmul_mx(
@@ -215,7 +224,7 @@ def tile_cptensorproduct_pa_kernel(tc, x1, A, t2, w, C, out):
 
         def contract_ranks(q):
             h_codes, h_scales = h_mx[q]
-            out_ps = out_psum.tile([P, D_ROWS, PAIR * CO], F32)
+            out_ps = psum.tile([P, D_ROWS, PAIR * CO], F32, tag="bank")
             for i in range(D_ROWS):
                 comps = slice(i * P, (i + 1) * P)
                 nc.tensor.matmul_mx(
@@ -234,8 +243,8 @@ def tile_cptensorproduct_pa_kernel(tc, x1, A, t2, w, C, out):
                 in_=out_sb[:].rearrange("p s i c -> p s (i c)"),
             )
 
-        def is_sample(b):
-            return 0 <= b < NB
+        def opens_group(b):
+            return is_sample(b) and b % GROUP == 0
 
         def closes_pair(b):
             return is_sample(b) and b % PAIR == PAIR - 1
@@ -243,12 +252,20 @@ def tile_cptensorproduct_pa_kernel(tc, x1, A, t2, w, C, out):
         for n in range(NB + AT_OUT):
             if is_sample(n - AT_MULTIPLY):
                 multiply(n - AT_MULTIPLY)
+            if n == ROUND_OF_C:
+                transpose_c()
+            if opens_group(n - AT_TRANSPOSE):
+                transpose_w((n - AT_TRANSPOSE) // GROUP)
             if is_sample(n - AT_TRANSPOSE):
-                transpose_operands(n - AT_TRANSPOSE)
+                transpose_t2(n - AT_TRANSPOSE)
             if is_sample(n - AT_PROJECT):
                 project(n - AT_PROJECT)
+            if n == ROUND_OF_C + 1:
+                quantise_c()
             if is_sample(n - AT_QUANTISE):
-                quantise_operands(n - AT_QUANTISE)
+                quantise_t2(n - AT_QUANTISE)
+            if opens_group(n - AT_QUANTISE):
+                quantise_w((n - AT_QUANTISE) // GROUP)
             if is_sample(n - AT_T3):
                 contract_channels(n - AT_T3)
             if closes_pair(n - AT_QUANTISE_H):

@@ -17,6 +17,8 @@ D_ROWS = D // P
 PAIR = 2
 GROUP = 4
 PSUM_BANKS = 8
+FIRST_CHUNKS = (0, 1)
+LAST_CHUNKS = (2, 3)
 
 FLOPS = 2 * NB * R * CO * (D + CV) + 2 * NB * D * CO * R
 
@@ -92,6 +94,7 @@ def tile_cptensorproduct_pa_kernel(tc, x1, A, t2, w, C, out):
         c_codes = consts.tile([P, D_ROWS * P], U32, align_bytes=64)
         c_scales = consts.tile([P, D_ROWS * P], U8, align_bytes=64)
 
+        t1_banks = {}
         t1_tiles = {}
         t2_grouped_tiles = {}
         w_grouped_tiles = {}
@@ -119,20 +122,24 @@ def tile_cptensorproduct_pa_kernel(tc, x1, A, t2, w, C, out):
         def quantise_c():
             nc.vector.quantize_mx(out=c_codes[:].bitcast(FP8X4), scales=c_scales[:], in_=c_grouped[:])
 
-        def project(b):
+        def project(b, chunks):
+            if chunks[0] == 0:
+                t1_ps = psum.tile([P, PACK, CO], F32, tag="bank")
+                t1_banks[b] = t1_ps
             x1_b = x1_tiles[b // GROUP][:, b % GROUP, :]
-            t1_ps = psum.tile([P, PACK, CO], F32, tag="bank")
-            for j in range(PACK):
+            for j in chunks:
                 for i in range(D_ROWS):
                     nc.tensor.matmul(
-                        out=t1_ps[:, j, :],
+                        out=t1_banks[b][:, j, :],
                         lhsT=a_chunks[:, i, j, :],
                         rhs=x1_b[:, i * CO : (i + 1) * CO],
                         start=(i == 0),
                         stop=(i == D_ROWS - 1),
                     )
+
+        def keep_t1(b):
             t1_sb = t1_pool.tile([P, CO, PACK], F32)
-            nc.scalar.copy(out=t1_sb[:], in_=t1_ps[:].rearrange("p j c -> p c j"))
+            nc.scalar.copy(out=t1_sb[:], in_=t1_banks[b][:].rearrange("p j c -> p c j"))
             t1_tiles[b] = t1_sb
 
         def transpose_w(g):
@@ -259,7 +266,7 @@ def tile_cptensorproduct_pa_kernel(tc, x1, A, t2, w, C, out):
             if is_sample(n - AT_TRANSPOSE):
                 transpose_t2(n - AT_TRANSPOSE)
             if is_sample(n - AT_PROJECT):
-                project(n - AT_PROJECT)
+                project(n - AT_PROJECT, FIRST_CHUNKS)
             if n == ROUND_OF_C + 1:
                 quantise_c()
             if is_sample(n - AT_QUANTISE):
@@ -272,3 +279,6 @@ def tile_cptensorproduct_pa_kernel(tc, x1, A, t2, w, C, out):
                 quantise_h((n - AT_QUANTISE_H) // PAIR)
             if closes_pair(n - AT_OUT):
                 contract_ranks((n - AT_OUT) // PAIR)
+            if is_sample(n - AT_PROJECT):
+                project(n - AT_PROJECT, LAST_CHUNKS)
+                keep_t1(n - AT_PROJECT)

@@ -14,11 +14,9 @@ P = 128
 PACK = 4
 HALVES = 2
 D_ROWS = D // P
-PAIR = 2
+RUN = 2
 GROUP = 4
 PSUM_BANKS = 8
-FIRST_CHUNKS = (0, 1)
-LAST_CHUNKS = (2, 3)
 
 FLOPS = 2 * NB * R * CO * (D + CV) + 2 * NB * D * CO * R
 
@@ -29,7 +27,7 @@ AT_T3 = 5
 AT_MULTIPLY = 6
 AT_QUANTISE_H = 7
 AT_OUT = 8
-ROUND_OF_C = 4
+ROUND_OF_C = 5
 
 
 def tile_cptensorproduct_pa_kernel(tc, x1, A, t2, w, C, out):
@@ -39,15 +37,21 @@ def tile_cptensorproduct_pa_kernel(tc, x1, A, t2, w, C, out):
         x1_pool = ctx.enter_context(tc.tile_pool(name="x1_pool", bufs=NB // GROUP))
         w_pool = ctx.enter_context(tc.tile_pool(name="w_pool", bufs=NB // GROUP))
         t2_pool = ctx.enter_context(tc.tile_pool(name="t2_pool", bufs=NB))
-        work = ctx.enter_context(tc.tile_pool(name="work", bufs=3))
+        work = ctx.enter_context(tc.tile_pool(name="work", bufs=4))
         t1_pool = ctx.enter_context(tc.tile_pool(name="t1_pool", bufs=AT_MULTIPLY - AT_PROJECT + 2))
-        out_pool = ctx.enter_context(tc.tile_pool(name="out_pool", bufs=NB // PAIR))
+        out_pool = ctx.enter_context(tc.tile_pool(name="out_pool", bufs=NB))
         psum = ctx.enter_context(tc.psum_pool(name="psum", bufs=PSUM_BANKS))
 
         ctx.enter_context(tc.manual_schedule())
 
         def is_sample(b):
             return 0 <= b < NB
+
+        def opens_run(b):
+            return is_sample(b) and b % RUN == 0
+
+        def opens_group(b):
+            return is_sample(b) and b % GROUP == 0
 
         x1_tiles = []
         w_tiles = []
@@ -58,7 +62,7 @@ def tile_cptensorproduct_pa_kernel(tc, x1, A, t2, w, C, out):
         nc.sync.dma_start(out=a_in[:], in_=A.rearrange("(p i) r -> p (i r)", i=D_ROWS))
         c_in = consts.tile([P, D_ROWS * R], BF16)
         for n in range(NB + AT_TRANSPOSE):
-            if is_sample(n - AT_PROJECT) and (n - AT_PROJECT) % GROUP == 0:
+            if opens_group(n - AT_PROJECT):
                 b = n - AT_PROJECT
                 x1_in = x1_pool.tile([P, GROUP, D_ROWS * CO], BF16)
                 nc.sync.dma_start(
@@ -68,18 +72,19 @@ def tile_cptensorproduct_pa_kernel(tc, x1, A, t2, w, C, out):
                 x1_tiles.append(x1_in)
             if n == ROUND_OF_C:
                 nc.sync.dma_start(out=c_in[:], in_=C.rearrange("(p i) r -> p (i r)", i=D_ROWS))
-            if is_sample(n - AT_TRANSPOSE):
+            if opens_group(n - AT_TRANSPOSE):
                 b = n - AT_TRANSPOSE
-                if b % GROUP == 0:
-                    w_in = w_pool.tile([P, PACK * CV], BF16)
-                    nc.sync.dma_start(
-                        out=w_in[:],
-                        in_=w_rows[b * CO : (b + GROUP) * CO].rearrange("(p i) v -> p (i v)", i=PACK),
-                    )
-                    w_tiles.append(w_in)
-                t2_in = t2_pool.tile([P, PACK * CV], BF16)
-                nc.sync.dma_start(out=t2_in[:], in_=t2[b].rearrange("(p j) v -> p (j v)", j=PACK))
-                t2_tiles.append(t2_in)
+                w_in = w_pool.tile([P, PACK * CV], BF16)
+                nc.sync.dma_start(
+                    out=w_in[:],
+                    in_=w_rows[b * CO : (b + GROUP) * CO].rearrange("(p i) v -> p (i v)", i=PACK),
+                )
+                w_tiles.append(w_in)
+            if opens_run(n - AT_TRANSPOSE):
+                for b in range(n - AT_TRANSPOSE, n - AT_TRANSPOSE + RUN):
+                    t2_in = t2_pool.tile([P, PACK * CV], BF16)
+                    nc.sync.dma_start(out=t2_in[:], in_=t2[b].rearrange("(p j) v -> p (j v)", j=PACK))
+                    t2_tiles.append(t2_in)
 
         ident = consts.tile([P, P], F32)
         make_identity(nc, ident[:])
@@ -94,7 +99,6 @@ def tile_cptensorproduct_pa_kernel(tc, x1, A, t2, w, C, out):
         c_codes = consts.tile([P, D_ROWS * P], U32, align_bytes=64)
         c_scales = consts.tile([P, D_ROWS * P], U8, align_bytes=64)
 
-        t1_banks = {}
         t1_tiles = {}
         t2_grouped_tiles = {}
         w_grouped_tiles = {}
@@ -122,24 +126,20 @@ def tile_cptensorproduct_pa_kernel(tc, x1, A, t2, w, C, out):
         def quantise_c():
             nc.vector.quantize_mx(out=c_codes[:].bitcast(FP8X4), scales=c_scales[:], in_=c_grouped[:])
 
-        def project(b, chunks):
-            if chunks[0] == 0:
-                t1_ps = psum.tile([P, PACK, CO], F32, tag="bank")
-                t1_banks[b] = t1_ps
+        def project(b):
             x1_b = x1_tiles[b // GROUP][:, b % GROUP, :]
-            for j in chunks:
+            t1_ps = psum.tile([P, PACK, CO], F32, tag="bank")
+            for j in range(PACK):
                 for i in range(D_ROWS):
                     nc.tensor.matmul(
-                        out=t1_banks[b][:, j, :],
+                        out=t1_ps[:, j, :],
                         lhsT=a_chunks[:, i, j, :],
                         rhs=x1_b[:, i * CO : (i + 1) * CO],
                         start=(i == 0),
                         stop=(i == D_ROWS - 1),
                     )
-
-        def keep_t1(b):
             t1_sb = t1_pool.tile([P, CO, PACK], F32)
-            nc.scalar.copy(out=t1_sb[:], in_=t1_banks[b][:].rearrange("p j c -> p c j"))
+            nc.scalar.copy(out=t1_sb[:], in_=t1_ps[:].rearrange("p j c -> p c j"))
             t1_tiles[b] = t1_sb
 
         def transpose_w(g):
@@ -209,29 +209,28 @@ def tile_cptensorproduct_pa_kernel(tc, x1, A, t2, w, C, out):
             t3_tiles[b] = t3_ps
 
         def multiply(b):
-            if b % PAIR == 0:
-                h_grouped = work.tile([P, PAIR, CO, PACK], BF16, align_bytes=64)
-                h_grouped_tiles[b // PAIR] = h_grouped
+            h_grouped = work.tile([P, CO, PACK], BF16, align_bytes=64)
             nc.vector.tensor_tensor(
-                out=h_grouped_tiles[b // PAIR][:, b % PAIR],
+                out=h_grouped[:],
                 in0=t1_tiles[b][:],
                 in1=t3_tiles[b][:].rearrange("p j c -> p c j"),
                 op=mybir.AluOpType.mult,
             )
+            h_grouped_tiles[b] = h_grouped
 
-        def quantise_h(q):
-            h_codes = work.tile([P, PAIR * CO], U32, align_bytes=64)
-            h_scales = work.tile([P, PAIR * CO], U8, align_bytes=64)
+        def quantise_h(b):
+            h_codes = work.tile([P, CO], U32, align_bytes=64)
+            h_scales = work.tile([P, CO], U8, align_bytes=64)
             nc.vector.quantize_mx(
                 out=h_codes[:].bitcast(FP8X4),
                 scales=h_scales[:],
-                in_=h_grouped_tiles[q][:].rearrange("p s c t -> p (s c t)"),
+                in_=h_grouped_tiles[b][:].rearrange("p c t -> p (c t)"),
             )
-            h_mx[q] = (h_codes, h_scales)
+            h_mx[b] = (h_codes, h_scales)
 
-        def contract_ranks(q):
-            h_codes, h_scales = h_mx[q]
-            out_ps = psum.tile([P, D_ROWS, PAIR * CO], F32, tag="bank")
+        def contract_ranks(b):
+            h_codes, h_scales = h_mx[b]
+            out_ps = psum.tile([P, D_ROWS, CO], F32, tag="bank")
             for i in range(D_ROWS):
                 comps = slice(i * P, (i + 1) * P)
                 nc.tensor.matmul_mx(
@@ -243,42 +242,34 @@ def tile_cptensorproduct_pa_kernel(tc, x1, A, t2, w, C, out):
                     start=True,
                     stop=True,
                 )
-            out_sb = out_pool.tile([P, PAIR, D_ROWS, CO], F32)
-            nc.scalar.copy(out=out_sb[:], in_=out_ps[:].rearrange("p i (s c) -> p s i c", s=PAIR))
+            out_sb = out_pool.tile([P, D_ROWS, CO], F32)
+            nc.scalar.copy(out=out_sb[:], in_=out_ps[:])
             nc.sync.dma_start(
-                out=out[q * PAIR : (q + 1) * PAIR].rearrange("s (p i) c -> p s (i c)", i=D_ROWS),
-                in_=out_sb[:].rearrange("p s i c -> p s (i c)"),
+                out=out[b].rearrange("(p i) c -> p (i c)", i=D_ROWS),
+                in_=out_sb[:].rearrange("p i c -> p (i c)"),
             )
 
-        def opens_group(b):
-            return is_sample(b) and b % GROUP == 0
-
-        def closes_pair(b):
-            return is_sample(b) and b % PAIR == PAIR - 1
-
         for n in range(NB + AT_OUT):
-            if is_sample(n - AT_MULTIPLY):
-                multiply(n - AT_MULTIPLY)
-            if n == ROUND_OF_C:
-                transpose_c()
-            if opens_group(n - AT_TRANSPOSE):
-                transpose_w((n - AT_TRANSPOSE) // GROUP)
-            if is_sample(n - AT_TRANSPOSE):
-                transpose_t2(n - AT_TRANSPOSE)
-            if is_sample(n - AT_PROJECT):
-                project(n - AT_PROJECT, FIRST_CHUNKS)
-            if n == ROUND_OF_C + 1:
-                quantise_c()
             if is_sample(n - AT_QUANTISE):
                 quantise_t2(n - AT_QUANTISE)
             if opens_group(n - AT_QUANTISE):
                 quantise_w((n - AT_QUANTISE) // GROUP)
+            if n == ROUND_OF_C + 1:
+                quantise_c()
+            if is_sample(n - AT_MULTIPLY):
+                multiply(n - AT_MULTIPLY)
+            if is_sample(n - AT_QUANTISE_H):
+                quantise_h(n - AT_QUANTISE_H)
+            if n == ROUND_OF_C:
+                transpose_c()
+            if opens_group(n - AT_TRANSPOSE):
+                transpose_w((n - AT_TRANSPOSE) // GROUP)
+            if opens_run(n - AT_TRANSPOSE):
+                for b in range(n - AT_TRANSPOSE, n - AT_TRANSPOSE + RUN):
+                    transpose_t2(b)
+            if is_sample(n - AT_PROJECT):
+                project(n - AT_PROJECT)
             if is_sample(n - AT_T3):
                 contract_channels(n - AT_T3)
-            if closes_pair(n - AT_QUANTISE_H):
-                quantise_h((n - AT_QUANTISE_H) // PAIR)
-            if closes_pair(n - AT_OUT):
-                contract_ranks((n - AT_OUT) // PAIR)
-            if is_sample(n - AT_PROJECT):
-                project(n - AT_PROJECT, LAST_CHUNKS)
-                keep_t1(n - AT_PROJECT)
+            if is_sample(n - AT_OUT):
+                contract_ranks(n - AT_OUT)

from contextlib import ExitStack

import concourse.mybir as mybir
from concourse.masks import make_identity

F32 = mybir.dt.float32
BF16 = mybir.dt.bfloat16
U32 = mybir.dt.uint32
U8 = mybir.dt.uint8
FP8X4 = mybir.dt.float8_e4m3fn_x4

NB, D, CO, CV, R = 16, 256, 128, 512, 512
P = 128
PACK = 4
HALVES = 2
D_ROWS = D // P
RUN = 2
GROUP = 4
PSUM_BANKS = 8

FLOPS = 2 * NB * R * CO * (D + CV) + 2 * NB * D * CO * R

AT_PROJECT = 0
AT_TRANSPOSE = 3
AT_QUANTISE = 4
AT_T3 = 5
AT_MULTIPLY = 6
AT_QUANTISE_H = 7
AT_OUT = 8
ROUND_OF_C = 5


def tile_cptensorproduct_pa_kernel(tc, x1, A, t2, w, C, out):
    nc = tc.nc
    with ExitStack() as ctx:
        consts = ctx.enter_context(tc.tile_pool(name="consts", bufs=1))
        x1_pool = ctx.enter_context(tc.tile_pool(name="x1_pool", bufs=NB // GROUP))
        w_pool = ctx.enter_context(tc.tile_pool(name="w_pool", bufs=NB // GROUP))
        t2_pool = ctx.enter_context(tc.tile_pool(name="t2_pool", bufs=NB))
        work = ctx.enter_context(tc.tile_pool(name="work", bufs=4))
        t1_pool = ctx.enter_context(tc.tile_pool(name="t1_pool", bufs=AT_MULTIPLY - AT_PROJECT + 2))
        out_pool = ctx.enter_context(tc.tile_pool(name="out_pool", bufs=NB))
        psum = ctx.enter_context(tc.psum_pool(name="psum", bufs=PSUM_BANKS))

        ctx.enter_context(tc.manual_schedule())

        def is_sample(b):
            return 0 <= b < NB

        def opens_run(b):
            return is_sample(b) and b % RUN == 0

        def opens_group(b):
            return is_sample(b) and b % GROUP == 0

        x1_tiles = []
        w_tiles = []
        t2_tiles = []
        w_rows = w.rearrange("b o v -> (b o) v")

        a_in = consts.tile([P, D_ROWS * R], BF16)
        nc.sync.dma_start(out=a_in[:], in_=A.rearrange("(p i) r -> p (i r)", i=D_ROWS))
        c_in = consts.tile([P, D_ROWS * R], BF16)
        for n in range(NB + AT_TRANSPOSE):
            if opens_group(n - AT_PROJECT):
                b = n - AT_PROJECT
                x1_in = x1_pool.tile([P, GROUP, D_ROWS * CO], BF16)
                nc.sync.dma_start(
                    out=x1_in[:],
                    in_=x1[b : b + GROUP].rearrange("b (p i) c -> p b (i c)", i=D_ROWS),
                )
                x1_tiles.append(x1_in)
            if n == ROUND_OF_C:
                nc.sync.dma_start(out=c_in[:], in_=C.rearrange("(p i) r -> p (i r)", i=D_ROWS))
            if opens_group(n - AT_TRANSPOSE):
                b = n - AT_TRANSPOSE
                w_in = w_pool.tile([P, PACK * CV], BF16)
                nc.sync.dma_start(
                    out=w_in[:],
                    in_=w_rows[b * CO : (b + GROUP) * CO].rearrange("(p i) v -> p (i v)", i=PACK),
                )
                w_tiles.append(w_in)
            if opens_run(n - AT_TRANSPOSE):
                for b in range(n - AT_TRANSPOSE, n - AT_TRANSPOSE + RUN):
                    t2_in = t2_pool.tile([P, PACK * CV], BF16)
                    nc.sync.dma_start(out=t2_in[:], in_=t2[b].rearrange("(p j) v -> p (j v)", j=PACK))
                    t2_tiles.append(t2_in)

        ident = consts.tile([P, P], F32)
        make_identity(nc, ident[:])

        a_chunks = consts.tile([P, D_ROWS, PACK, P], BF16)
        nc.vector.tensor_copy(
            out=a_chunks[:],
            in_=a_in[:].rearrange("p (i m j) -> p i j m", i=D_ROWS, j=PACK),
        )

        c_grouped = consts.tile([P, D_ROWS * P * PACK], BF16, align_bytes=64)
        c_codes = consts.tile([P, D_ROWS * P], U32, align_bytes=64)
        c_scales = consts.tile([P, D_ROWS * P], U8, align_bytes=64)

        t1_tiles = {}
        t2_grouped_tiles = {}
        w_grouped_tiles = {}
        t2_mx = {}
        w_mx = {}
        t3_tiles = {}
        h_grouped_tiles = {}
        h_mx = {}

        def transpose_c():
            c_words = c_in[:].bitcast(F32)
            cT_ps = psum.tile([P, D_ROWS, HALVES, P], F32, tag="bank")
            for i in range(D_ROWS):
                for u in range(HALVES):
                    nc.tensor.transpose(
                        cT_ps[:, i, u, :],
                        c_words[:, i * (R // 2) + u : (i + 1) * (R // 2) : 2],
                        ident[:],
                    )
            nc.vector.tensor_copy(
                out=c_grouped[:].bitcast(F32).rearrange("p (i d u) -> p i d u", i=D_ROWS, u=HALVES),
                in_=cT_ps[:].rearrange("p i u d -> p i d u"),
            )

        def quantise_c():
            nc.vector.quantize_mx(out=c_codes[:].bitcast(FP8X4), scales=c_scales[:], in_=c_grouped[:])

        def project(b):
            x1_b = x1_tiles[b // GROUP][:, b % GROUP, :]
            t1_ps = psum.tile([P, PACK, CO], F32, tag="bank")
            for j in range(PACK):
                for i in range(D_ROWS):
                    nc.tensor.matmul(
                        out=t1_ps[:, j, :],
                        lhsT=a_chunks[:, i, j, :],
                        rhs=x1_b[:, i * CO : (i + 1) * CO],
                        start=(i == 0),
                        stop=(i == D_ROWS - 1),
                    )
            t1_sb = t1_pool.tile([P, CO, PACK], F32)
            nc.scalar.copy(out=t1_sb[:], in_=t1_ps[:].rearrange("p j c -> p c j"))
            t1_tiles[b] = t1_sb

        def transpose_w(g):
            w_words = w_tiles[g][:].bitcast(F32)
            w_grouped = work.tile([P, GROUP * CO * PACK], BF16, align_bytes=64)
            grouped_words = w_grouped[:].bitcast(F32).rearrange("p (q i u) -> p q i u", i=PACK, u=HALVES)
            for k in range(PACK // 2):
                wT_ps = psum.tile([P, 2, HALVES, P], F32, tag="bank")
                for ii in range(2):
                    for u in range(HALVES):
                        first = ((2 * k + ii) * HALVES + u) * P
                        nc.tensor.transpose(wT_ps[:, ii, u, :], w_words[:, first : first + P], ident[:])
                nc.vector.tensor_copy(
                    out=grouped_words[:, :, 2 * k : 2 * k + 2, :],
                    in_=wT_ps[:].rearrange("p ii u q -> p q ii u"),
                )
            w_grouped_tiles[g] = w_grouped

        def transpose_t2(b):
            t2_words = t2_tiles[b][:].bitcast(F32)
            t2_grouped = work.tile([P, PACK * P * PACK], BF16, align_bytes=64)
            grouped_words = t2_grouped[:].bitcast(F32).rearrange("p (j m u) -> p j m u", j=PACK, u=HALVES)
            for k in range(PACK // 2):
                t2T_ps = psum.tile([P, 2, HALVES, P], F32, tag="bank")
                for jj in range(2):
                    for u in range(HALVES):
                        first = ((2 * k + jj) * HALVES + u) * P
                        nc.tensor.transpose(t2T_ps[:, jj, u, :], t2_words[:, first : first + P], ident[:])
                nc.scalar.copy(
                    out=grouped_words[:, 2 * k : 2 * k + 2],
                    in_=t2T_ps[:].rearrange("p jj u m -> p jj m u"),
                )
            t2_grouped_tiles[b] = t2_grouped

        def quantise_t2(b):
            t2_codes = work.tile([P, PACK * P], U32, align_bytes=64)
            t2_scales = work.tile([P, PACK * P], U8, align_bytes=64)
            nc.vector.quantize_mx(
                out=t2_codes[:].bitcast(FP8X4), scales=t2_scales[:], in_=t2_grouped_tiles[b][:]
            )
            t2_mx[b] = (t2_codes, t2_scales)

        def quantise_w(g):
            w_codes = work.tile([P, GROUP * CO], U32, align_bytes=64)
            w_scales = work.tile([P, GROUP * CO], U8, align_bytes=64)
            nc.vector.quantize_mx(
                out=w_codes[:].bitcast(FP8X4), scales=w_scales[:], in_=w_grouped_tiles[g][:]
            )
            w_mx[g] = (w_codes, w_scales)

        def contract_channels(b):
            t2_codes, t2_scales = t2_mx[b]
            w_codes, w_scales = w_mx[b // GROUP]
            w_cols = slice((b % GROUP) * CO, (b % GROUP + 1) * CO)
            t3_ps = psum.tile([P, PACK, CO], F32, tag="bank")
            for j in range(PACK):
                ranks = slice(j * P, (j + 1) * P)
                nc.tensor.matmul_mx(
                    out=t3_ps[:, j, :],
                    lhsT=t2_codes[:, ranks].bitcast(FP8X4),
                    lhsT_scale=t2_scales[:, ranks],
                    rhs=w_codes[:, w_cols].bitcast(FP8X4),
                    rhs_scale=w_scales[:, w_cols],
                    start=True,
                    stop=True,
                )
            t3_tiles[b] = t3_ps

        def multiply(b):
            h_grouped = work.tile([P, CO, PACK], BF16, align_bytes=64)
            nc.vector.tensor_tensor(
                out=h_grouped[:],
                in0=t1_tiles[b][:],
                in1=t3_tiles[b][:].rearrange("p j c -> p c j"),
                op=mybir.AluOpType.mult,
            )
            h_grouped_tiles[b] = h_grouped

        def quantise_h(b):
            h_codes = work.tile([P, CO], U32, align_bytes=64)
            h_scales = work.tile([P, CO], U8, align_bytes=64)
            nc.vector.quantize_mx(
                out=h_codes[:].bitcast(FP8X4),
                scales=h_scales[:],
                in_=h_grouped_tiles[b][:].rearrange("p c t -> p (c t)"),
            )
            h_mx[b] = (h_codes, h_scales)

        def contract_ranks(b):
            h_codes, h_scales = h_mx[b]
            out_ps = psum.tile([P, D_ROWS, CO], F32, tag="bank")
            for i in range(D_ROWS):
                comps = slice(i * P, (i + 1) * P)
                nc.tensor.matmul_mx(
                    out=out_ps[:, i, :],
                    lhsT=c_codes[:, comps].bitcast(FP8X4),
                    lhsT_scale=c_scales[:, comps],
                    rhs=h_codes[:].bitcast(FP8X4),
                    rhs_scale=h_scales[:],
                    start=True,
                    stop=True,
                )
            out_sb = out_pool.tile([P, D_ROWS, CO], F32)
            nc.scalar.copy(out=out_sb[:], in_=out_ps[:])
            nc.sync.dma_start(
                out=out[b].rearrange("(p i) c -> p (i c)", i=D_ROWS),
                in_=out_sb[:].rearrange("p i c -> p (i c)"),
            )

        for n in range(NB + AT_OUT):
            if is_sample(n - AT_QUANTISE):
                quantise_t2(n - AT_QUANTISE)
            if opens_group(n - AT_QUANTISE):
                quantise_w((n - AT_QUANTISE) // GROUP)
            if n == ROUND_OF_C + 1:
                quantise_c()
            if is_sample(n - AT_MULTIPLY):
                multiply(n - AT_MULTIPLY)
            if is_sample(n - AT_QUANTISE_H):
                quantise_h(n - AT_QUANTISE_H)
            if n == ROUND_OF_C:
                transpose_c()
            if opens_group(n - AT_TRANSPOSE):
                transpose_w((n - AT_TRANSPOSE) // GROUP)
            if opens_run(n - AT_TRANSPOSE):
                for b in range(n - AT_TRANSPOSE, n - AT_TRANSPOSE + RUN):
                    transpose_t2(b)
            if is_sample(n - AT_PROJECT):
                project(n - AT_PROJECT)
            if is_sample(n - AT_T3):
                contract_channels(n - AT_T3)
            if is_sample(n - AT_OUT):
                contract_ranks(n - AT_OUT)
